import numpy as np
import ml_dtypes


def mxq(x, axis, fmt="e4m3"):
    dtype, down = {"e4m3": (ml_dtypes.float8_e4m3fn, 7), "e5m2": (ml_dtypes.float8_e5m2, 14)}[fmt]
    v = np.moveaxis(np.asarray(x, np.float32).astype(ml_dtypes.bfloat16).astype(np.float64), axis, -1)
    blocks = v.reshape(v.shape[:-1] + (-1, 32))
    amax = np.abs(blocks).max(-1, keepdims=True)
    byte = np.maximum(np.where(amax > 0, np.frexp(amax)[1] - 1 + 127, 0) - down, 1)
    scale = np.exp2(byte - 127.0)
    codes = (blocks / scale).astype(np.float32).astype(dtype).astype(np.float64)
    return np.moveaxis((codes * scale).reshape(v.shape), -1, axis)


WIDE = False


def mx_kscale(k):
    if not WIDE:
        return np.ones(k)
    levels = np.array([10, -10, 5, -5, 0])
    if k % 512:
        return np.exp2(np.random.permutation(np.resize(levels, k // 32))).repeat(32)
    a = np.empty((k // 512, 16))
    for p in range(k // 512):
        a[p, :8] = np.random.permutation(np.resize(levels, 8))
        for g in range(8):
            far = levels[np.abs(levels - a[p, g]) >= 10]
            a[p, g + 8] = far[np.random.randint(len(far))]
    return np.exp2(a.ravel()).repeat(32)


BF16 = ml_dtypes.bfloat16


def bf(x):
    return np.asarray(x, np.float32).astype(BF16)


def f64(x):
    return np.asarray(x).astype(np.float64)


B, T, D, H, HD = 4, 2048, 512, 2, 64
E = H * HD
HALF = HD // 2


def rotate_half(u):
    return np.concatenate((-u[..., HALF:], u[..., :HALF]), axis=-1)


def setup_inputs():
    s = mx_kscale(D)
    return {"x": bf(np.random.standard_normal((B, T, D)) * s),
            "rope_cos": bf(np.random.random_sample((1, 1, T, HD))),
            "rope_sin": bf(np.random.random_sample((1, 1, T, HD))),
            "qkv_w": bf(np.random.standard_normal((3 * E, D)) / np.sqrt(D) / s[None, :]),
            "qkv_b": bf(np.random.standard_normal(3 * E) * 0.3)}


def reference(x, rope_cos, rope_sin, qkv_w, qkv_b):
    qkv = (mxq(f64(x), 2, "e4m3") @ mxq(f64(qkv_w), 1, "e4m3").T) + f64(qkv_b)
    qkv = qkv.reshape(B, T, 3, H, HD).transpose(2, 0, 3, 1, 4)
    q, k, v = qkv[0], qkv[1], qkv[2]
    cos = f64(rope_cos)[:, :, :T, :]
    sin = f64(rope_sin)[:, :, :T, :]
    q_rot = q * cos + rotate_half(q) * sin
    k_rot = k * cos + rotate_half(k) * sin
    return q_rot, k_rot, v

@@ -1,0 +1,255 @@
+from contextlib import ExitStack
+
+import concourse.mybir as mybir
+from concourse.masks import make_identity
+
+F32 = mybir.dt.float32
+BF16 = mybir.dt.bfloat16
+U32 = mybir.dt.uint32
+U8 = mybir.dt.uint8
+FP8X4 = mybir.dt.float8_e4m3fn_x4
+ALU = mybir.AluOpType
+ACT = mybir.ActivationFunctionType
+
+P = 128
+B, T, D, H, HD = 4, 2048, 512, 2, 64
+HALF = HD // 2
+FLOPS = 2 * B * T * D * 3 * H * HD
+
+JS = 8
+JG = 4
+N_GROUPS = B * T // (P * JG)
+
+
+def tile_causalselfattention_pa_t_kernel(
+    tc, x, rope_cos, rope_sin, qkv_w, qkv_b, out_0, out_1, out_2
+):
+    nc = tc.nc
+    outs = [out_0, out_1, out_2]
+    with ExitStack() as ctx:
+        ctx.enter_context(tc.manual_schedule())
+        const = ctx.enter_context(tc.tile_pool(name="const", bufs=1))
+        xin = ctx.enter_context(tc.tile_pool(name="xin", bufs=N_GROUPS))
+        grp = ctx.enter_context(tc.tile_pool(name="grp", bufs=3))
+        cod = ctx.enter_context(tc.tile_pool(name="cod", bufs=3))
+        qbp = ctx.enter_context(tc.tile_pool(name="qbp", bufs=2))
+        mp = ctx.enter_context(tc.tile_pool(name="mp", bufs=4))
+        stp = ctx.enter_context(tc.tile_pool(name="stp", bufs=3))
+        ps_xt = ctx.enter_context(tc.psum_pool(name="ps_xt", bufs=2))
+        ps_acc = ctx.enter_context(tc.psum_pool(name="ps_acc", bufs=3))
+        ps_qk = ctx.enter_context(tc.psum_pool(name="ps_qk", bufs=2))
+        ps_vb = ctx.enter_context(tc.psum_pool(name="ps_vb", bufs=1))
+
+        b_rows = const.tile([P, P], BF16, name="b_rows")
+        nc.vector.memset(b_rows[:], 0.0)
+        ident = const.tile([P, P], F32, name="ident")
+        make_identity(nc, ident[:])
+
+        w_sb = const.tile([P, 3 * D], BF16, name="w_sb")
+        nc.sync.dma_start(
+            out=w_sb[:].rearrange("f (m k) -> f m k", m=3),
+            in_=qkv_w.rearrange("(m f) k -> f m k", m=3),
+        )
+        x_sb = []
+
+        def load_x(g):
+            b, blk, j0 = g // 4, (g // 2) % 2, JG * (g % 2)
+            xt_sb = xin.tile([P, JG * D], BF16, name="x_sb")
+            rows = x[b, blk * P * JS : (blk + 1) * P * JS, :].rearrange("(p j) k -> p j k", j=JS)
+            nc.sync.dma_start(
+                out=xt_sb[:].rearrange("p (j k) -> p j k", j=JG), in_=rows[:, j0 : j0 + JG, :]
+            )
+            x_sb.append(xt_sb)
+
+        load_x(0)
+        nc.sync.dma_start(out=b_rows[0:3, :], in_=qkv_b.rearrange("(m f) -> m f", m=3))
+        cos_sb = const.tile([P, 2, JS, HD], BF16, name="cos_sb")
+        sin_sb = const.tile([P, 2, JS, HD], BF16, name="sin_sb")
+        nc.sync.dma_start(out=cos_sb[:], in_=rope_cos[0, 0].rearrange("(s p j) d -> p s j d", s=2, j=JS))
+        nc.sync.dma_start(out=sin_sb[:], in_=rope_sin[0, 0].rearrange("(s p j) d -> p s j d", s=2, j=JS))
+        for g in range(1, N_GROUPS):
+            load_x(g)
+
+        w_words = w_sb[:].bitcast(F32)
+        w_grouped = const.tile([P, 3 * P * 4], BF16, name="w_grouped", align_bytes=64)
+        wg_words = w_grouped[:].bitcast(F32).rearrange("p (t u) -> p t u", u=2)
+        w_codes = const.tile([P, 3 * P], U32, name="w_codes", align_bytes=64)
+        w_scales = const.tile([P, 3 * P], U8, name="w_scales", align_bytes=64)
+        wt0 = ps_xt.tile([P, 2, 2, P], F32, name="xt")
+        for m in range(2):
+            for u in range(2):
+                c0 = m * 256
+                nc.tensor.transpose(wt0[:, m, u, :], w_words[:, c0 + u : c0 + 256 : 2], ident[:])
+        nc.vector.tensor_copy(
+            out=wg_words[:, 0 : 2 * P, :].rearrange("p (j t) u -> p j t u", j=2),
+            in_=wt0[:].rearrange("p j u t -> p j t u"),
+        )
+        wt1 = ps_xt.tile([P, 2, 2, P], F32, name="xt")
+        for u in range(2):
+            c0 = 2 * 256
+            nc.tensor.transpose(wt1[:, 0, u, :], w_words[:, c0 + u : c0 + 256 : 2], ident[:])
+        nc.vector.tensor_copy(
+            out=wg_words[:, 2 * P : 3 * P, :], in_=wt1[:, 0].rearrange("p u t -> p t u")
+        )
+        nc.vector.quantize_mx(
+            out=w_codes[:, 0 : 2 * P].bitcast(FP8X4),
+            scales=w_scales[:, 0 : 2 * P],
+            in_=w_grouped[:, 0 : 2 * P * 4],
+        )
+        nc.vector.quantize_mx(
+            out=w_codes[:, 2 * P : 3 * P].bitcast(FP8X4),
+            scales=w_scales[:, 2 * P : 3 * P],
+            in_=w_grouped[:, 2 * P * 4 : 3 * P * 4],
+        )
+
+        bias_sb = const.tile([P, 4], F32, name="bias_sb")
+        sin_x = const.tile([P, 2, JS, HD], F32, name="sin_x")
+        cos_f = const.tile([P, 2, JS, HD], F32, name="cos_f")
+
+        def small_tables():
+            b_f32 = const.tile([P, P], F32, name="b_f32")
+            nc.vector.tensor_copy(out=b_f32[:], in_=b_rows[:])
+            bt = ps_xt.tile([P, 2, 2, P], F32, name="xt")
+            nc.tensor.transpose(bt[:, 0, 0, :], b_f32[:], ident[:])
+            nc.vector.tensor_copy(out=bias_sb[:, 0:3], in_=bt[:, 0, 0, 0:3])
+            nc.vector.tensor_copy(out=cos_f[:], in_=cos_sb[:])
+            nc.vector.tensor_copy(out=sin_x[:, :, :, 0:HALF], in_=sin_sb[:, :, :, HALF:HD])
+            nc.vector.tensor_scalar_mul(
+                out=sin_x[:, :, :, HALF:HD], in0=sin_sb[:, :, :, 0:HALF], scalar1=-1.0
+            )
+
+        grouped_t = {}
+        codes_t = {}
+        qb_t = {}
+        stg_t = {}
+
+        def stage_a(g):
+            x_words = x_sb[g][:].bitcast(F32)
+            grouped = grp.tile([P, JG * P * 4], BF16, name="grouped", align_bytes=64)
+            g_words = grouped[:].bitcast(F32).rearrange("p (t u) -> p t u", u=2)
+            for pr in range(2):
+                xt = ps_xt.tile([P, 2, 2, P], F32, name="xt")
+                for jj in range(2):
+                    for u in range(2):
+                        c0 = (2 * pr + jj) * 256
+                        nc.tensor.transpose(xt[:, jj, u, :], x_words[:, c0 + u : c0 + 256 : 2], ident[:])
+                dst = g_words[:, pr * 2 * P : (pr + 1) * 2 * P, :].rearrange(
+                    "p (j t) u -> p j t u", j=2
+                )
+                src = xt[:].rearrange("p j u t -> p j t u")
+                nc.scalar.copy(out=dst, in_=src)
+            grouped_t[g] = grouped
+
+        def stage_b(g):
+            codes = cod.tile([P, JG * P], U32, name="codes", align_bytes=64)
+            scales = cod.tile([P, JG * P], U8, name="scales", align_bytes=64)
+            nc.vector.quantize_mx(
+                out=codes[:].bitcast(FP8X4), scales=scales[:], in_=grouped_t[g][:]
+            )
+            codes_t[g] = (codes, scales)
+
+        def stage_c(g):
+            codes, scales = codes_t[g]
+            accs = []
+            for m in range(3):
+                acc = ps_acc.tile([P, JG * P], F32, name="acc")
+                nc.tensor.matmul_mx(
+                    out=acc[:],
+                    lhsT=w_codes[:, m * P : (m + 1) * P].bitcast(FP8X4),
+                    lhsT_scale=w_scales[:, m * P : (m + 1) * P],
+                    rhs=codes[:].bitcast(FP8X4),
+                    rhs_scale=scales[:],
+                    start=True,
+                    stop=True,
+                )
+                accs.append(acc)
+            qbs = []
+            for m in range(3):
+                qb = qbp.tile([P, JG * P], F32, name="qb%d" % m)
+                nc.scalar.activation(
+                    out=qb[:], in_=accs[m][:], func=ACT.Identity, bias=bias_sb[:, m : m + 1], scale=1.0
+                )
+                qbs.append(qb)
+            qb_t[g] = qbs
+
+        def stage_d(g):
+            b, blk, j0 = g // 4, (g // 2) % 2, JG * (g % 2)
+            qbs = qb_t[g]
+            if g % 2 == 0:
+                stg_new = stp.tile([P, 3, H, JS, HD], F32, name="stg")
+                stg_t[g // 2] = stg_new
+            stg = stg_t[g // 2]
+            qks = []
+            for pr in range(2):
+                qk = ps_qk.tile([P, 2, 2, P], F32, name="qk")
+                for jj in range(2):
+                    for m in range(2):
+                        c0 = (2 * pr + jj) * P
+                        nc.tensor.transpose(qk[:, jj, m, :], qbs[m][:, c0 : c0 + P], ident[:])
+                qks.append(qk)
+            vb = ps_vb.tile([P, JG, P], F32, name="vb")
+            for jj in range(JG):
+                nc.tensor.transpose(vb[:, jj, :], qbs[2][:, jj * P : (jj + 1) * P], ident[:])
+            nc.scalar.copy(
+                out=stg[:, 2, :, j0 : j0 + JG, :].rearrange("p h j d -> p j h d"),
+                in_=vb[:].rearrange("p j (h d) -> p j h d", h=H),
+            )
+            last_block = g // 2 == N_GROUPS // 2 - 1
+
+            def store(s, ja, jn):
+                dram = outs[s][b, :, blk * P * JS : (blk + 1) * P * JS, :].rearrange(
+                    "h (p j) d -> p h j d", j=JS
+                )
+                nc.sync.dma_start(out=dram[:, :, ja : ja + jn, :], in_=stg[:, s, :, ja : ja + jn, :])
+
+            if last_block:
+                store(2, j0, JG)
+            stg_qk = stg[:, 0:2].rearrange("p s h j d -> p j (s h) d")
+            for pr in range(2):
+                jl = j0 + 2 * pr
+                u_ps = qks[pr][:].rearrange("p j m (h d) -> p j (m h) d", h=H)
+                m1 = mp.tile([P, 2, 2 * H, HD], F32, name="m1")
+                m2 = mp.tile([P, 2, 2 * H, HD], F32, name="m2")
+                shape = [P, 2, 2 * H, HD]
+                nc.vector.tensor_tensor(
+                    out=m1[:],
+                    in0=u_ps,
+                    in1=cos_f[:, blk, jl : jl + 2, :].unsqueeze(2).to_broadcast(shape),
+                    op=ALU.mult,
+                )
+                nc.vector.tensor_tensor(
+                    out=m2[:],
+                    in0=u_ps,
+                    in1=sin_x[:, blk, jl : jl + 2, :].unsqueeze(2).to_broadcast(shape),
+                    op=ALU.mult,
+                )
+                for hf in range(2):
+                    lo, ol = hf * HALF, (1 - hf) * HALF
+                    adder = nc.vector if (g == N_GROUPS - 1 and pr == 1) else nc.gpsimd
+                    adder.tensor_tensor(
+                        out=stg_qk[:, jl : jl + 2, :, lo : lo + HALF],
+                        in0=m1[:, :, :, lo : lo + HALF],
+                        in1=m2[:, :, :, ol : ol + HALF],
+                        op=ALU.add,
+                    )
+                if g == N_GROUPS - 1:
+                    store(0, jl, 2)
+                    store(1, jl, 2)
+            if g == N_GROUPS - 2:
+                store(0, j0, JG)
+                store(1, j0, JG)
+            if g % 2 == 1 and not last_block:
+                for s in range(3):
+                    store(s, 0, JS)
+
+        for it in range(-2, N_GROUPS + 1):
+            if 0 <= it - 1:
+                stage_d(it - 1)
+            if 0 <= it < N_GROUPS:
+                stage_c(it)
+            if it + 2 < N_GROUPS:
+                stage_a(it + 2)
+            if 0 <= it + 1 < N_GROUPS:
+                stage_b(it + 1)
+            if it == -1:
+                small_tables()

@@ -148,37 +148,34 @@ def tile_causalselfattention_pa_t_kernel(
             )
             codes_t[g] = (codes, scales)
 
-        def stage_c(g):
+        def stage_c(g, ms):
             codes, scales = codes_t[g]
-            accs = []
-            for m in range(3):
+            qbs = qb_t.setdefault(g, {})
+            accs = {}
+            for m in ms:
                 acc = ps_acc.tile([P, JG * P], F32, name="acc")
-                nc.tensor.matmul_mx(
-                    out=acc[:],
-                    lhsT=w_codes[:, m * P : (m + 1) * P].bitcast(FP8X4),
-                    lhsT_scale=w_scales[:, m * P : (m + 1) * P],
-                    rhs=codes[:].bitcast(FP8X4),
-                    rhs_scale=scales[:],
-                    start=True,
-                    stop=True,
-                )
-                accs.append(acc)
-            qbs = []
-            for m in range(3):
+                for rep in range(2 if m == 2 else 1):
+                    nc.tensor.matmul_mx(
+                        out=acc[:],
+                        lhsT=w_codes[:, m * P : (m + 1) * P].bitcast(FP8X4),
+                        lhsT_scale=w_scales[:, m * P : (m + 1) * P],
+                        rhs=codes[:].bitcast(FP8X4),
+                        rhs_scale=scales[:],
+                        start=True,
+                        stop=True,
+                    )
+                accs[m] = acc
+            for m in ms:
                 qb = qbp.tile([P, JG * P], F32, name="qb%d" % m)
                 nc.scalar.activation(
                     out=qb[:], in_=accs[m][:], func=ACT.Identity, bias=bias_sb[:, m : m + 1], scale=1.0
                 )
-                qbs.append(qb)
-            qb_t[g] = qbs
+                qbs[m] = qb
 
-        def stage_d(g):
-            b, blk, j0 = g // 4, (g // 2) % 2, JG * (g % 2)
+        qks_t = {}
+
+        def stage_d1(g):
             qbs = qb_t[g]
-            if g % 2 == 0:
-                stg_new = stp.tile([P, 3, H, JS, HD], F32, name="stg")
-                stg_t[g // 2] = stg_new
-            stg = stg_t[g // 2]
             qks = []
             for pr in range(2):
                 qk = ps_qk.tile([P, 2, 2, P], F32, name="qk")
@@ -187,6 +184,16 @@ def tile_causalselfattention_pa_t_kernel(
                         c0 = (2 * pr + jj) * P
                         nc.tensor.transpose(qk[:, jj, m, :], qbs[m][:, c0 : c0 + P], ident[:])
                 qks.append(qk)
+            qks_t[g] = qks
+
+        def stage_d2(g):
+            b, blk, j0 = g // 4, (g // 2) % 2, JG * (g % 2)
+            qbs = qb_t[g]
+            qks = qks_t[g]
+            if g % 2 == 0:
+                stg_new = stp.tile([P, 3, H, JS, HD], F32, name="stg")
+                stg_t[g // 2] = stg_new
+            stg = stg_t[g // 2]
             vb = ps_vb.tile([P, JG, P], F32, name="vb")
             for jj in range(JG):
                 nc.tensor.transpose(vb[:, jj, :], qbs[2][:, jj * P : (jj + 1) * P], ident[:])
@@ -244,11 +251,15 @@ def tile_causalselfattention_pa_t_kernel(
 
         for it in range(-2, N_GROUPS + 1):
             if 0 <= it - 1:
-                stage_d(it - 1)
+                stage_d1(it - 1)
             if 0 <= it < N_GROUPS:
-                stage_c(it)
+                stage_c(it, (0, 1))
+            if 0 <= it - 1:
+                stage_d2(it - 1)
             if it + 2 < N_GROUPS:
                 stage_a(it + 2)
+            if 0 <= it < N_GROUPS:
+                stage_c(it, (2,))
             if 0 <= it + 1 < N_GROUPS:
                 stage_b(it + 1)
             if it == -1:

@@ -45,6 +45,18 @@ def tile_causalselfattention_pa_t_kernel(
         ident = const.tile([P, P], F32, name="ident")
         make_identity(nc, ident[:])
 
+        zeros = const.tile([P, JG * P], BF16, name="zeros")
+        nc.vector.memset(zeros[:], 0.0)
+
+        def warm_up(n):
+            wm = ps_vb.tile([P, JG, P], F32, name="vb")
+            for rep in range(n):
+                nc.tensor.matmul(
+                    wm[:].rearrange("p j t -> p (j t)"), lhsT=zeros[:, 0:P], rhs=zeros[:], start=True, stop=True
+                )
+
+        warm_up(5)
+
         w_sb = const.tile([P, 3 * D], BF16, name="w_sb")
         nc.sync.dma_start(
             out=w_sb[:].rearrange("f (m k) -> f m k", m=3),
@@ -123,22 +135,19 @@ def tile_causalselfattention_pa_t_kernel(
         qb_t = {}
         stg_t = {}
 
-        def stage_a(g):
+        def stage_a(g, pr):
+            if pr == 0:
+                grouped_new = grp.tile([P, JG * P * 4], BF16, name="grouped", align_bytes=64)
+                grouped_t[g] = grouped_new
             x_words = x_sb[g][:].bitcast(F32)
-            grouped = grp.tile([P, JG * P * 4], BF16, name="grouped", align_bytes=64)
-            g_words = grouped[:].bitcast(F32).rearrange("p (t u) -> p t u", u=2)
-            for pr in range(2):
-                xt = ps_xt.tile([P, 2, 2, P], F32, name="xt")
-                for jj in range(2):
-                    for u in range(2):
-                        c0 = (2 * pr + jj) * 256
-                        nc.tensor.transpose(xt[:, jj, u, :], x_words[:, c0 + u : c0 + 256 : 2], ident[:])
-                dst = g_words[:, pr * 2 * P : (pr + 1) * 2 * P, :].rearrange(
-                    "p (j t) u -> p j t u", j=2
-                )
-                src = xt[:].rearrange("p j u t -> p j t u")
-                nc.scalar.copy(out=dst, in_=src)
-            grouped_t[g] = grouped
+            g_words = grouped_t[g][:].bitcast(F32).rearrange("p (t u) -> p t u", u=2)
+            xt = ps_xt.tile([P, 2, 2, P], F32, name="xt")
+            for jj in range(2):
+                for u in range(2):
+                    c0 = (2 * pr + jj) * 256
+                    nc.tensor.transpose(xt[:, jj, u, :], x_words[:, c0 + u : c0 + 256 : 2], ident[:])
+            dst = g_words[:, pr * 2 * P : (pr + 1) * 2 * P, :].rearrange("p (j t) u -> p j t u", j=2)
+            nc.scalar.copy(out=dst, in_=xt[:].rearrange("p j u t -> p j t u"))
 
         def stage_b(g):
             codes = cod.tile([P, JG * P], U32, name="codes", align_bytes=64)
@@ -249,6 +258,7 @@ def tile_causalselfattention_pa_t_kernel(
                 for s in range(3):
                     store(s, 0, JS)
 
+        warm_up(2)
         for it in range(-2, N_GROUPS + 1):
             if 0 <= it - 1:
                 stage_d1(it - 1)
@@ -257,9 +267,15 @@ def tile_causalselfattention_pa_t_kernel(
             if 0 <= it - 1:
                 stage_d2(it - 1)
             if it + 2 < N_GROUPS:
-                stage_a(it + 2)
+                stage_a(it + 2, 0)
+            if it < 0:
+                warm_up(2)
             if 0 <= it < N_GROUPS:
                 stage_c(it, (2,))
+            if it + 2 < N_GROUPS:
+                stage_a(it + 2, 1)
+            if it < 0:
+                warm_up(2)
             if 0 <= it + 1 < N_GROUPS:
                 stage_b(it + 1)
             if it == -1:

@@ -220,34 +220,37 @@ def tile_causalselfattention_pa_t_kernel(
 
             if last_block:
                 store(2, j0, JG)
-            stg_qk = stg[:, 0:2].rearrange("p s h j d -> p j (s h) d")
+            stg_qk = stg[:, 0:2].rearrange("p s h j d -> p (s h) j d")
             for pr in range(2):
                 jl = j0 + 2 * pr
                 u_ps = qks[pr][:].rearrange("p j m (h d) -> p j (m h) d", h=H)
-                m1 = mp.tile([P, 2, 2 * H, HD], F32, name="m1")
-                m2 = mp.tile([P, 2, 2 * H, HD], F32, name="m2")
-                shape = [P, 2, 2 * H, HD]
+                m1 = mp.tile([P, 2 * H, 2, HD], F32, name="m1")
+                m2 = mp.tile([P, 2 * H, 2, HD], F32, name="m2")
+                m1_v = m1[:].rearrange("p s j d -> p j s d")
+                m2_v = m2[:].rearrange("p s j d -> p j s d")
                 nc.vector.tensor_tensor(
-                    out=m1[:],
+                    out=m1_v,
                     in0=u_ps,
-                    in1=cos_f[:, blk, jl : jl + 2, :].unsqueeze(2).to_broadcast(shape),
-                    op=ALU.mult,
-                )
-                nc.vector.tensor_tensor(
-                    out=m2[:],
-                    in0=u_ps,
-                    in1=sin_x[:, blk, jl : jl + 2, :].unsqueeze(2).to_broadcast(shape),
+                    in1=cos_f[:, blk, jl : jl + 2, :].unsqueeze(2).to_broadcast([P, 2, 2 * H, HD]),
                     op=ALU.mult,
                 )
                 for hf in range(2):
                     lo, ol = hf * HALF, (1 - hf) * HALF
-                    adder = nc.vector if (g == N_GROUPS - 1 and pr == 1) else nc.gpsimd
-                    adder.tensor_tensor(
-                        out=stg_qk[:, jl : jl + 2, :, lo : lo + HALF],
-                        in0=m1[:, :, :, lo : lo + HALF],
-                        in1=m2[:, :, :, ol : ol + HALF],
-                        op=ALU.add,
+                    nc.vector.tensor_tensor(
+                        out=m2_v[:, :, :, ol : ol + HALF],
+                        in0=u_ps[:, :, :, lo : lo + HALF],
+                        in1=sin_x[:, blk, jl : jl + 2, lo : lo + HALF]
+                        .unsqueeze(2)
+                        .to_broadcast([P, 2, 2 * H, HALF]),
+                        op=ALU.mult,
                     )
+                adder = nc.vector if (g == N_GROUPS - 1 and pr == 1) else nc.gpsimd
+                adder.tensor_tensor(
+                    out=stg_qk[:, :, jl : jl + 2, :].rearrange("p s j d -> p s (j d)"),
+                    in0=m1[:].rearrange("p s j d -> p s (j d)"),
+                    in1=m2[:].rearrange("p s j d -> p s (j d)"),
+                    op=ALU.add,
+                )
                 if g == N_GROUPS - 1:
                     store(0, jl, 2)
                     store(1, jl, 2)

@@ -19,6 +19,8 @@ FLOPS = 2 * B * T * D * 3 * H * HD
 JS = 8
 JG = 4
 N_GROUPS = B * T // (P * JG)
+SLOTS = T // (P * JG)
+N_TILES = T // P
 
 
 def tile_causalselfattention_pa_t_kernel(
@@ -32,13 +34,11 @@ def tile_causalselfattention_pa_t_kernel(
         xin = ctx.enter_context(tc.tile_pool(name="xin", bufs=N_GROUPS))
         grp = ctx.enter_context(tc.tile_pool(name="grp", bufs=3))
         cod = ctx.enter_context(tc.tile_pool(name="cod", bufs=3))
-        qbp = ctx.enter_context(tc.tile_pool(name="qbp", bufs=2))
-        mp = ctx.enter_context(tc.tile_pool(name="mp", bufs=4))
+        mid = ctx.enter_context(tc.tile_pool(name="mid", bufs=3))
         stp = ctx.enter_context(tc.tile_pool(name="stp", bufs=3))
         ps_xt = ctx.enter_context(tc.psum_pool(name="ps_xt", bufs=2))
         ps_acc = ctx.enter_context(tc.psum_pool(name="ps_acc", bufs=3))
-        ps_qk = ctx.enter_context(tc.psum_pool(name="ps_qk", bufs=2))
-        ps_vb = ctx.enter_context(tc.psum_pool(name="ps_vb", bufs=1))
+        ps_o = ctx.enter_context(tc.psum_pool(name="ps_o", bufs=1))
 
         b_rows = const.tile([P, P], BF16, name="b_rows")
         nc.vector.memset(b_rows[:], 0.0)
@@ -49,19 +49,14 @@ def tile_causalselfattention_pa_t_kernel(
         nc.vector.memset(zeros[:], 0.0)
 
         def warm_up(n):
-            wm = ps_vb.tile([P, JG, P], F32, name="vb")
+            wm = ps_o.tile([P, JG, P], F32, name="turned2")
             for rep in range(n):
                 nc.tensor.matmul(
                     wm[:].rearrange("p j t -> p (j t)"), lhsT=zeros[:, 0:P], rhs=zeros[:], start=True, stop=True
                 )
 
-        warm_up(5)
+        warm_up(3)
 
-        w_sb = const.tile([P, 3 * D], BF16, name="w_sb")
-        nc.sync.dma_start(
-            out=w_sb[:].rearrange("f (m k) -> f m k", m=3),
-            in_=qkv_w.rearrange("(m f) k -> f m k", m=3),
-        )
         x_sb = []
 
         def load_x(g):
@@ -71,80 +66,108 @@ def tile_causalselfattention_pa_t_kernel(
             nc.sync.dma_start(
                 out=xt_sb[:].rearrange("p (j k) -> p j k", j=JG), in_=rows[:, j0 : j0 + JG, :]
             )
-            x_sb.append(xt_sb)
+            x_sb.append((xt_sb[:, 0 : 2 * D], xt_sb[:, 2 * D : 4 * D]))
 
-        load_x(0)
+        def load_x_half(pr):
+            half = const.tile([P, 2 * D], BF16, name="x_half%d" % pr)
+            rows = x[0, 0 : P * JS, :].rearrange("(p j) k -> p j k", j=JS)
+            nc.sync.dma_start(
+                out=half[:].rearrange("p (j k) -> p j k", j=2), in_=rows[:, 2 * pr : 2 * pr + 2, :]
+            )
+            return half[:]
+
+        x_half0 = load_x_half(0)
+        w_sb = const.tile([P, 3 * D], BF16, name="w_sb")
+        nc.sync.dma_start(
+            out=w_sb[:].rearrange("f (m k) -> f m k", m=3),
+            in_=qkv_w.rearrange("(m f) k -> f m k", m=3),
+        )
+        x_half1 = load_x_half(1)
+        x_sb.append((x_half0, x_half1))
         nc.sync.dma_start(out=b_rows[0:3, :], in_=qkv_b.rearrange("(m f) -> m f", m=3))
-        cos_sb = const.tile([P, 2, JS, HD], BF16, name="cos_sb")
-        sin_sb = const.tile([P, 2, JS, HD], BF16, name="sin_sb")
-        nc.sync.dma_start(out=cos_sb[:], in_=rope_cos[0, 0].rearrange("(s p j) d -> p s j d", s=2, j=JS))
-        nc.sync.dma_start(out=sin_sb[:], in_=rope_sin[0, 0].rearrange("(s p j) d -> p s j d", s=2, j=JS))
-        for g in range(1, N_GROUPS):
+        for g in (1, 2):
+            load_x(g)
+        cos_sb = const.tile([P, N_TILES, HD], BF16, name="cos_sb")
+        sin_sb = const.tile([P, N_TILES, HD], BF16, name="sin_sb")
+        for tab, src in ((cos_sb, rope_cos), (sin_sb, rope_sin)):
+            nc.sync.dma_start(
+                out=tab[:].rearrange("p (s j) d -> p s j d", s=2),
+                in_=src[0, 0].rearrange("(s p j) d -> p s j d", s=2, j=JS),
+            )
+        for g in range(3, N_GROUPS):
             load_x(g)
 
+        b_f32 = const.tile([P, P], F32, name="b_f32")
         w_words = w_sb[:].bitcast(F32)
         w_grouped = const.tile([P, 3 * P * 4], BF16, name="w_grouped", align_bytes=64)
         wg_words = w_grouped[:].bitcast(F32).rearrange("p (t u) -> p t u", u=2)
         w_codes = const.tile([P, 3 * P], U32, name="w_codes", align_bytes=64)
         w_scales = const.tile([P, 3 * P], U8, name="w_scales", align_bytes=64)
-        wt0 = ps_xt.tile([P, 2, 2, P], F32, name="xt")
-        for m in range(2):
-            for u in range(2):
-                c0 = m * 256
-                nc.tensor.transpose(wt0[:, m, u, :], w_words[:, c0 + u : c0 + 256 : 2], ident[:])
-        nc.vector.tensor_copy(
-            out=wg_words[:, 0 : 2 * P, :].rearrange("p (j t) u -> p j t u", j=2),
-            in_=wt0[:].rearrange("p j u t -> p j t u"),
-        )
-        wt1 = ps_xt.tile([P, 2, 2, P], F32, name="xt")
-        for u in range(2):
-            c0 = 2 * 256
-            nc.tensor.transpose(wt1[:, 0, u, :], w_words[:, c0 + u : c0 + 256 : 2], ident[:])
-        nc.vector.tensor_copy(
-            out=wg_words[:, 2 * P : 3 * P, :], in_=wt1[:, 0].rearrange("p u t -> p t u")
-        )
-        nc.vector.quantize_mx(
-            out=w_codes[:, 0 : 2 * P].bitcast(FP8X4),
-            scales=w_scales[:, 0 : 2 * P],
-            in_=w_grouped[:, 0 : 2 * P * 4],
-        )
-        nc.vector.quantize_mx(
-            out=w_codes[:, 2 * P : 3 * P].bitcast(FP8X4),
-            scales=w_scales[:, 2 * P : 3 * P],
-            in_=w_grouped[:, 2 * P * 4 : 3 * P * 4],
-        )
+
+        def weights():
+            wt0 = ps_acc.tile([P, 2, 2, P], F32, name="acc")
+            wt1 = ps_acc.tile([P, 2, 2, P], F32, name="acc")
+            for m in range(3):
+                for u in range(2):
+                    c0 = m * 256
+                    dst = wt0[:, m, u, :] if m < 2 else wt1[:, 0, u, :]
+                    nc.tensor.transpose(dst, w_words[:, c0 + u : c0 + 256 : 2], ident[:])
+            nc.vector.tensor_copy(
+                out=wg_words[:, 0 : 2 * P, :].rearrange("p (j t) u -> p j t u", j=2),
+                in_=wt0[:].rearrange("p j u t -> p j t u"),
+            )
+            nc.vector.tensor_copy(
+                out=wg_words[:, 2 * P : 3 * P, :], in_=wt1[:, 0].rearrange("p u t -> p t u")
+            )
+            nc.vector.tensor_copy(out=b_f32[:], in_=b_rows[:])
+            nc.vector.quantize_mx(
+                out=w_codes[:, 0 : 2 * P].bitcast(FP8X4),
+                scales=w_scales[:, 0 : 2 * P],
+                in_=w_grouped[:, 0 : 2 * P * 4],
+            )
+            nc.vector.quantize_mx(
+                out=w_codes[:, 2 * P : 3 * P].bitcast(FP8X4),
+                scales=w_scales[:, 2 * P : 3 * P],
+                in_=w_grouped[:, 2 * P * 4 : 3 * P * 4],
+            )
 
         bias_sb = const.tile([P, 4], F32, name="bias_sb")
-        sin_x = const.tile([P, 2, JS, HD], F32, name="sin_x")
-        cos_f = const.tile([P, 2, JS, HD], F32, name="cos_f")
 
-        def small_tables():
-            b_f32 = const.tile([P, P], F32, name="b_f32")
-            nc.vector.tensor_copy(out=b_f32[:], in_=b_rows[:])
-            bt = ps_xt.tile([P, 2, 2, P], F32, name="xt")
+        def bias_column():
+            bt = ps_acc.tile([P, 2, 2, P], F32, name="acc")
             nc.tensor.transpose(bt[:, 0, 0, :], b_f32[:], ident[:])
             nc.vector.tensor_copy(out=bias_sb[:, 0:3], in_=bt[:, 0, 0, 0:3])
-            nc.vector.tensor_copy(out=cos_f[:], in_=cos_sb[:])
-            nc.vector.tensor_copy(out=sin_x[:, :, :, 0:HALF], in_=sin_sb[:, :, :, HALF:HD])
+
+        cos_d = const.tile([P, N_TILES, H, HD], BF16, name="cos_d")
+        sin_d = const.tile([P, N_TILES, H, HD], BF16, name="sin_d")
+
+        def rope_tables():
+            def both_heads(tab):
+                return tab.unsqueeze(2).to_broadcast([P, N_TILES, H, tab.shape[2]])
+
+            nc.vector.tensor_copy(out=cos_d[:], in_=both_heads(cos_sb[:]))
+            nc.vector.tensor_copy(out=sin_d[:, :, :, 0:HALF], in_=both_heads(sin_sb[:, :, HALF:HD]))
             nc.vector.tensor_scalar_mul(
-                out=sin_x[:, :, :, HALF:HD], in0=sin_sb[:, :, :, 0:HALF], scalar1=-1.0
+                out=sin_d[:, :, :, HALF:HD], in0=both_heads(sin_sb[:, :, 0:HALF]), scalar1=-1.0
             )
 
         grouped_t = {}
         codes_t = {}
-        qb_t = {}
+        acc_t = {}
+        biased_t = {}
+        turned_t = {}
         stg_t = {}
 
         def stage_a(g, pr):
             if pr == 0:
                 grouped_new = grp.tile([P, JG * P * 4], BF16, name="grouped", align_bytes=64)
                 grouped_t[g] = grouped_new
-            x_words = x_sb[g][:].bitcast(F32)
+            x_words = x_sb[g][pr].bitcast(F32)
             g_words = grouped_t[g][:].bitcast(F32).rearrange("p (t u) -> p t u", u=2)
             xt = ps_xt.tile([P, 2, 2, P], F32, name="xt")
             for jj in range(2):
                 for u in range(2):
-                    c0 = (2 * pr + jj) * 256
+                    c0 = jj * 256
                     nc.tensor.transpose(xt[:, jj, u, :], x_words[:, c0 + u : c0 + 256 : 2], ident[:])
             dst = g_words[:, pr * 2 * P : (pr + 1) * 2 * P, :].rearrange("p (j t) u -> p j t u", j=2)
             nc.scalar.copy(out=dst, in_=xt[:].rearrange("p j u t -> p j t u"))
@@ -157,129 +180,114 @@ def tile_causalselfattention_pa_t_kernel(
             )
             codes_t[g] = (codes, scales)
 
-        def stage_c(g, ms):
+        def passes(g):
             codes, scales = codes_t[g]
-            qbs = qb_t.setdefault(g, {})
-            accs = {}
-            for m in ms:
+            for m in range(3):
                 acc = ps_acc.tile([P, JG * P], F32, name="acc")
-                for rep in range(2 if m == 2 else 1):
-                    nc.tensor.matmul_mx(
-                        out=acc[:],
-                        lhsT=w_codes[:, m * P : (m + 1) * P].bitcast(FP8X4),
-                        lhsT_scale=w_scales[:, m * P : (m + 1) * P],
-                        rhs=codes[:].bitcast(FP8X4),
-                        rhs_scale=scales[:],
-                        start=True,
-                        stop=True,
-                    )
-                accs[m] = acc
-            for m in ms:
-                qb = qbp.tile([P, JG * P], F32, name="qb%d" % m)
-                nc.scalar.activation(
-                    out=qb[:], in_=accs[m][:], func=ACT.Identity, bias=bias_sb[:, m : m + 1], scale=1.0
+                nc.tensor.matmul_mx(
+                    out=acc[:],
+                    lhsT=w_codes[:, m * P : (m + 1) * P].bitcast(FP8X4),
+                    lhsT_scale=w_scales[:, m * P : (m + 1) * P],
+                    rhs=codes[:].bitcast(FP8X4),
+                    rhs_scale=scales[:],
+                    start=True,
+                    stop=True,
                 )
-                qbs[m] = qb
+                acc_t[g, m] = acc
 
-        qks_t = {}
+        def place(g):
+            return g // 4, (g // 2) % 2, JG * (g % 2)
 
-        def stage_d1(g):
-            qbs = qb_t[g]
-            qks = []
-            for pr in range(2):
-                qk = ps_qk.tile([P, 2, 2, P], F32, name="qk")
-                for jj in range(2):
-                    for m in range(2):
-                        c0 = (2 * pr + jj) * P
-                        nc.tensor.transpose(qk[:, jj, m, :], qbs[m][:, c0 : c0 + P], ident[:])
-                qks.append(qk)
-            qks_t[g] = qks
+        def add_bias(g, m):
+            biased = mid.tile([P, JG * P], F32, name="biased%d" % m)
+            if m < 2:
+                nc.scalar.activation(
+                    out=biased[:], in_=acc_t[g, m][:], func=ACT.Identity, bias=bias_sb[:, m : m + 1], scale=1.0
+                )
+            else:
+                nc.vector.tensor_scalar_add(
+                    out=biased[:], in0=acc_t[g, m][:], scalar1=bias_sb[:, m : m + 1]
+                )
+            biased_t[g, m] = biased
 
-        def stage_d2(g):
-            b, blk, j0 = g // 4, (g // 2) % 2, JG * (g % 2)
-            qbs = qb_t[g]
-            qks = qks_t[g]
-            if g % 2 == 0:
-                stg_new = stp.tile([P, 3, H, JS, HD], F32, name="stg")
-                stg_t[g // 2] = stg_new
-            stg = stg_t[g // 2]
-            vb = ps_vb.tile([P, JG, P], F32, name="vb")
+        def turn(g, m):
+            turned = ps_o.tile([P, JG, P], F32, name="turned%d" % m)
             for jj in range(JG):
-                nc.tensor.transpose(vb[:, jj, :], qbs[2][:, jj * P : (jj + 1) * P], ident[:])
-            nc.scalar.copy(
-                out=stg[:, 2, :, j0 : j0 + JG, :].rearrange("p h j d -> p j h d"),
-                in_=vb[:].rearrange("p j (h d) -> p j h d", h=H),
-            )
-            last_block = g // 2 == N_GROUPS // 2 - 1
+                nc.tensor.transpose(turned[:, jj, :], biased_t[g, m][:, jj * P : (jj + 1) * P], ident[:])
+            turned_t[g, m] = turned
 
-            def store(s, ja, jn):
+        def staged(g, m):
+            j0 = place(g)[2]
+            return stg_t[g // 2][:, m, :, j0 : j0 + JG, :].rearrange("p h j d -> p j h d")
+
+        def rotate(g, m):
+            i0 = (g % SLOTS) * JG
+            u_ps = turned_t[g, m][:].rearrange("p j (h d) -> p (j h) d", h=H)
+            cos_i = cos_d[:, i0 : i0 + JG].rearrange("p j h d -> p (j h) d")
+            sin_i = sin_d[:, i0 : i0 + JG].rearrange("p j h d -> p (j h) d")
+            m1 = mid.tile([P, JG * H, HD], F32, name="m1")
+            m2 = mid.tile([P, JG * H, HD], F32, name="m2")
+            nc.vector.tensor_tensor(out=m1[:], in0=u_ps, in1=cos_i, op=ALU.mult)
+            nc.vector.tensor_tensor(
+                out=m2[:].rearrange("p i (f d) -> p i f d", f=2),
+                in0=u_ps.rearrange("p i (f d) -> p i f d", f=2)[:, :, ::-1, :],
+                in1=sin_i.rearrange("p i (f d) -> p i f d", f=2)[:, :, ::-1, :],
+                op=ALU.mult,
+            )
+            adder = nc.vector if g == N_GROUPS - 1 and m == 1 else nc.gpsimd
+            adder.tensor_tensor(
+                out=staged(g, m),
+                in0=m1[:].rearrange("p (j h) d -> p j h d", h=H),
+                in1=m2[:].rearrange("p (j h) d -> p j h d", h=H),
+                op=ALU.add,
+            )
+
+        def copy_v(g):
+            nc.scalar.copy(out=staged(g, 2), in_=turned_t[g, 2][:].rearrange("p j (h d) -> p j h d", h=H))
+
+        def stores(g):
+            b, blk, j0 = place(g)
+            stg = stg_t[g // 2]
+            last_block = g // 2 == N_GROUPS // 2 - 1
+            if g % 2 == 0 and not last_block:
+                return
+            ja, jn = (j0, JG) if last_block else (0, JS)
+            for s in (2, 0, 1):
                 dram = outs[s][b, :, blk * P * JS : (blk + 1) * P * JS, :].rearrange(
                     "h (p j) d -> p h j d", j=JS
                 )
                 nc.sync.dma_start(out=dram[:, :, ja : ja + jn, :], in_=stg[:, s, :, ja : ja + jn, :])
 
-            if last_block:
-                store(2, j0, JG)
-            stg_qk = stg[:, 0:2].rearrange("p s h j d -> p (s h) j d")
-            for pr in range(2):
-                jl = j0 + 2 * pr
-                u_ps = qks[pr][:].rearrange("p j m (h d) -> p j (m h) d", h=H)
-                m1 = mp.tile([P, 2 * H, 2, HD], F32, name="m1")
-                m2 = mp.tile([P, 2 * H, 2, HD], F32, name="m2")
-                m1_v = m1[:].rearrange("p s j d -> p j s d")
-                m2_v = m2[:].rearrange("p s j d -> p j s d")
-                nc.vector.tensor_tensor(
-                    out=m1_v,
-                    in0=u_ps,
-                    in1=cos_f[:, blk, jl : jl + 2, :].unsqueeze(2).to_broadcast([P, 2, 2 * H, HD]),
-                    op=ALU.mult,
-                )
-                for hf in range(2):
-                    lo, ol = hf * HALF, (1 - hf) * HALF
-                    nc.vector.tensor_tensor(
-                        out=m2_v[:, :, :, ol : ol + HALF],
-                        in0=u_ps[:, :, :, lo : lo + HALF],
-                        in1=sin_x[:, blk, jl : jl + 2, lo : lo + HALF]
-                        .unsqueeze(2)
-                        .to_broadcast([P, 2, 2 * H, HALF]),
-                        op=ALU.mult,
-                    )
-                adder = nc.vector if (g == N_GROUPS - 1 and pr == 1) else nc.gpsimd
-                adder.tensor_tensor(
-                    out=stg_qk[:, :, jl : jl + 2, :].rearrange("p s j d -> p s (j d)"),
-                    in0=m1[:].rearrange("p s j d -> p s (j d)"),
-                    in1=m2[:].rearrange("p s j d -> p s (j d)"),
-                    op=ALU.add,
-                )
-                if g == N_GROUPS - 1:
-                    store(0, jl, 2)
-                    store(1, jl, 2)
-            if g == N_GROUPS - 2:
-                store(0, j0, JG)
-                store(1, j0, JG)
-            if g % 2 == 1 and not last_block:
-                for s in range(3):
-                    store(s, 0, JS)
-
-        warm_up(2)
-        for it in range(-2, N_GROUPS + 1):
-            if 0 <= it - 1:
-                stage_d1(it - 1)
-            if 0 <= it < N_GROUPS:
-                stage_c(it, (0, 1))
-            if 0 <= it - 1:
-                stage_d2(it - 1)
+        stage_a(0, 0)
+        weights()
+        stage_a(0, 1)
+        warm_up(1)
+        stage_b(0)
+        stage_a(1, 0)
+        bias_column()
+        stage_a(1, 1)
+        for it in range(N_GROUPS + 1):
+            if it == 1:
+                rope_tables()
+            if it > 0:
+                if it % 2 == 1:
+                    stg_new = stp.tile([P, 3, H, JS, HD], F32, name="stg")
+                    stg_t[it // 2] = stg_new
+                turn(it - 1, 0)
+                turn(it - 1, 1)
+                rotate(it - 1, 0)
+            if it + 1 < N_GROUPS:
+                stage_b(it + 1)
+            if it > 0:
+                rotate(it - 1, 1)
+            if it < N_GROUPS:
+                passes(it)
+                for m in range(3):
+                    add_bias(it, m)
+            if it > 0:
+                turn(it - 1, 2)
+                copy_v(it - 1)
+                stores(it - 1)
             if it + 2 < N_GROUPS:
                 stage_a(it + 2, 0)
-            if it < 0:
-                warm_up(2)
-            if 0 <= it < N_GROUPS:
-                stage_c(it, (2,))
-            if it + 2 < N_GROUPS:
                 stage_a(it + 2, 1)
-            if it < 0:
-                warm_up(2)
-            if 0 <= it + 1 < N_GROUPS:
-                stage_b(it + 1)
-            if it == -1:
-                small_tables()

@@ -37,8 +37,8 @@ def tile_causalselfattention_pa_t_kernel(
         mid = ctx.enter_context(tc.tile_pool(name="mid", bufs=3))
         stp = ctx.enter_context(tc.tile_pool(name="stp", bufs=3))
         ps_xt = ctx.enter_context(tc.psum_pool(name="ps_xt", bufs=2))
-        ps_acc = ctx.enter_context(tc.psum_pool(name="ps_acc", bufs=3))
-        ps_o = ctx.enter_context(tc.psum_pool(name="ps_o", bufs=1))
+        ps_acc = ctx.enter_context(tc.psum_pool(name="ps_acc", bufs=2))
+        ps_o = ctx.enter_context(tc.psum_pool(name="ps_o", bufs=4))
 
         b_rows = const.tile([P, P], BF16, name="b_rows")
         nc.vector.memset(b_rows[:], 0.0)
@@ -49,10 +49,10 @@ def tile_causalselfattention_pa_t_kernel(
         nc.vector.memset(zeros[:], 0.0)
 
         def warm_up(n):
-            wm = ps_o.tile([P, JG, P], F32, name="turned2")
+            wm = ps_o.tile([P, H, JG, HD], F32, name="turned")
             for rep in range(n):
                 nc.tensor.matmul(
-                    wm[:].rearrange("p j t -> p (j t)"), lhsT=zeros[:, 0:P], rhs=zeros[:], start=True, stop=True
+                    wm[:].rearrange("p h j d -> p (h j d)"), lhsT=zeros[:, 0:P], rhs=zeros[:], start=True, stop=True
                 )
 
         warm_up(3)
@@ -76,17 +76,16 @@ def tile_causalselfattention_pa_t_kernel(
             )
             return half[:]
 
-        x_half0 = load_x_half(0)
         w_sb = const.tile([P, 3 * D], BF16, name="w_sb")
         nc.sync.dma_start(
             out=w_sb[:].rearrange("f (m k) -> f m k", m=3),
             in_=qkv_w.rearrange("(m f) k -> f m k", m=3),
         )
+        x_half0 = load_x_half(0)
         x_half1 = load_x_half(1)
         x_sb.append((x_half0, x_half1))
         nc.sync.dma_start(out=b_rows[0:3, :], in_=qkv_b.rearrange("(m f) -> m f", m=3))
-        for g in (1, 2):
-            load_x(g)
+        load_x(1)
         cos_sb = const.tile([P, N_TILES, HD], BF16, name="cos_sb")
         sin_sb = const.tile([P, N_TILES, HD], BF16, name="sin_sb")
         for tab, src in ((cos_sb, rope_cos), (sin_sb, rope_sin)):
@@ -94,7 +93,7 @@ def tile_causalselfattention_pa_t_kernel(
                 out=tab[:].rearrange("p (s j) d -> p s j d", s=2),
                 in_=src[0, 0].rearrange("(s p j) d -> p s j d", s=2, j=JS),
             )
-        for g in range(3, N_GROUPS):
+        for g in range(2, N_GROUPS):
             load_x(g)
 
         b_f32 = const.tile([P, P], F32, name="b_f32")
@@ -116,9 +115,7 @@ def tile_causalselfattention_pa_t_kernel(
                 out=wg_words[:, 0 : 2 * P, :].rearrange("p (j t) u -> p j t u", j=2),
                 in_=wt0[:].rearrange("p j u t -> p j t u"),
             )
-            nc.vector.tensor_copy(
-                out=wg_words[:, 2 * P : 3 * P, :], in_=wt1[:, 0].rearrange("p u t -> p t u")
-            )
+            nc.scalar.copy(out=wg_words[:, 2 * P : 3 * P, :], in_=wt1[:, 0].rearrange("p u t -> p t u"))
             nc.vector.tensor_copy(out=b_f32[:], in_=b_rows[:])
             nc.vector.quantize_mx(
                 out=w_codes[:, 0 : 2 * P].bitcast(FP8X4),
@@ -138,18 +135,19 @@ def tile_causalselfattention_pa_t_kernel(
             nc.tensor.transpose(bt[:, 0, 0, :], b_f32[:], ident[:])
             nc.vector.tensor_copy(out=bias_sb[:, 0:3], in_=bt[:, 0, 0, 0:3])
 
-        cos_d = const.tile([P, N_TILES, H, HD], BF16, name="cos_d")
-        sin_d = const.tile([P, N_TILES, H, HD], BF16, name="sin_d")
+        rope = const.tile([P, 2, SLOTS, H, JG, HD], BF16, name="rope")
 
         def rope_tables():
-            def both_heads(tab):
-                return tab.unsqueeze(2).to_broadcast([P, N_TILES, H, tab.shape[2]])
-
-            nc.vector.tensor_copy(out=cos_d[:], in_=both_heads(cos_sb[:]))
-            nc.vector.tensor_copy(out=sin_d[:, :, :, 0:HALF], in_=both_heads(sin_sb[:, :, HALF:HD]))
-            nc.vector.tensor_scalar_mul(
-                out=sin_d[:, :, :, HALF:HD], in0=both_heads(sin_sb[:, :, 0:HALF]), scalar1=-1.0
-            )
+            for h in range(H):
+                cos_h, sin_h = (rope[:, c, :, h] for c in range(2))
+                cos_v, sin_v = (
+                    tab[:].rearrange("p (s j) d -> p s j d", s=SLOTS) for tab in (cos_sb, sin_sb)
+                )
+                nc.vector.tensor_copy(out=cos_h, in_=cos_v)
+                nc.vector.tensor_copy(out=sin_h[:, :, :, 0:HALF], in_=sin_v[:, :, :, HALF:HD])
+                nc.vector.tensor_scalar_mul(
+                    out=sin_h[:, :, :, HALF:HD], in0=sin_v[:, :, :, 0:HALF], scalar1=-1.0
+                )
 
         grouped_t = {}
         codes_t = {}
@@ -175,14 +173,20 @@ def tile_causalselfattention_pa_t_kernel(
         def stage_b(g):
             codes = cod.tile([P, JG * P], U32, name="codes", align_bytes=64)
             scales = cod.tile([P, JG * P], U8, name="scales", align_bytes=64)
-            nc.vector.quantize_mx(
-                out=codes[:].bitcast(FP8X4), scales=scales[:], in_=grouped_t[g][:]
-            )
+            parts = 2 if g == 0 else 1
+            n = JG * P // parts
+            for i in range(parts):
+                cols = slice(i * n, (i + 1) * n)
+                nc.vector.quantize_mx(
+                    out=codes[:, cols].bitcast(FP8X4),
+                    scales=scales[:, cols],
+                    in_=grouped_t[g][:, i * 4 * n : (i + 1) * 4 * n],
+                )
             codes_t[g] = (codes, scales)
 
-        def passes(g):
+        def passes(g, ms):
             codes, scales = codes_t[g]
-            for m in range(3):
+            for m in ms:
                 acc = ps_acc.tile([P, JG * P], F32, name="acc")
                 nc.tensor.matmul_mx(
                     out=acc[:],
@@ -200,7 +204,7 @@ def tile_causalselfattention_pa_t_kernel(
 
         def add_bias(g, m):
             biased = mid.tile([P, JG * P], F32, name="biased%d" % m)
-            if m < 2:
+            if m < 2 or g % 2 == 1 or g == 0:
                 nc.scalar.activation(
                     out=biased[:], in_=acc_t[g, m][:], func=ACT.Identity, bias=bias_sb[:, m : m + 1], scale=1.0
                 )
@@ -211,39 +215,34 @@ def tile_causalselfattention_pa_t_kernel(
             biased_t[g, m] = biased
 
         def turn(g, m):
-            turned = ps_o.tile([P, JG, P], F32, name="turned%d" % m)
+            turned = ps_o.tile([P, H, JG, HD], F32, name="turned")
             for jj in range(JG):
-                nc.tensor.transpose(turned[:, jj, :], biased_t[g, m][:, jj * P : (jj + 1) * P], ident[:])
+                nc.tensor.transpose(turned[:, :, jj, :], biased_t[g, m][:, jj * P : (jj + 1) * P], ident[:])
             turned_t[g, m] = turned
 
         def staged(g, m):
             j0 = place(g)[2]
-            return stg_t[g // 2][:, m, :, j0 : j0 + JG, :].rearrange("p h j d -> p j h d")
+            return stg_t[g // 2][:, m, :, j0 : j0 + JG, :].rearrange("p h j d -> p h (j d)")
 
         def rotate(g, m):
-            i0 = (g % SLOTS) * JG
-            u_ps = turned_t[g, m][:].rearrange("p j (h d) -> p (j h) d", h=H)
-            cos_i = cos_d[:, i0 : i0 + JG].rearrange("p j h d -> p (j h) d")
-            sin_i = sin_d[:, i0 : i0 + JG].rearrange("p j h d -> p (j h) d")
-            m1 = mid.tile([P, JG * H, HD], F32, name="m1")
-            m2 = mid.tile([P, JG * H, HD], F32, name="m2")
+            u_ps = turned_t[g, m][:].rearrange("p h j d -> p h (j d)")
+            cos_i, sin_i = (
+                rope[:, c, g % SLOTS].rearrange("p h j d -> p h (j d)") for c in range(2)
+            )
+            m1 = mid.tile([P, H, JG * HD], F32, name="m1")
+            m2 = mid.tile([P, H, JG * HD], F32, name="m2")
             nc.vector.tensor_tensor(out=m1[:], in0=u_ps, in1=cos_i, op=ALU.mult)
             nc.vector.tensor_tensor(
-                out=m2[:].rearrange("p i (f d) -> p i f d", f=2),
-                in0=u_ps.rearrange("p i (f d) -> p i f d", f=2)[:, :, ::-1, :],
-                in1=sin_i.rearrange("p i (f d) -> p i f d", f=2)[:, :, ::-1, :],
+                out=m2[:].rearrange("p h (j f d) -> p h j f d", j=JG, f=2),
+                in0=u_ps.rearrange("p h (j f d) -> p h j f d", j=JG, f=2)[:, :, :, ::-1, :],
+                in1=sin_i.rearrange("p h (j f d) -> p h j f d", j=JG, f=2)[:, :, :, ::-1, :],
                 op=ALU.mult,
             )
             adder = nc.vector if g == N_GROUPS - 1 and m == 1 else nc.gpsimd
-            adder.tensor_tensor(
-                out=staged(g, m),
-                in0=m1[:].rearrange("p (j h) d -> p j h d", h=H),
-                in1=m2[:].rearrange("p (j h) d -> p j h d", h=H),
-                op=ALU.add,
-            )
+            adder.tensor_tensor(out=staged(g, m), in0=m1[:], in1=m2[:], op=ALU.add)
 
         def copy_v(g):
-            nc.scalar.copy(out=staged(g, 2), in_=turned_t[g, 2][:].rearrange("p j (h d) -> p j h d", h=H))
+            nc.scalar.copy(out=staged(g, 2), in_=turned_t[g, 2][:].rearrange("p h j d -> p h (j d)"))
 
         def stores(g):
             b, blk, j0 = place(g)
@@ -258,36 +257,44 @@ def tile_causalselfattention_pa_t_kernel(
                 )
                 nc.sync.dma_start(out=dram[:, :, ja : ja + jn, :], in_=stg[:, s, :, ja : ja + jn, :])
 
-        stage_a(0, 0)
         weights()
+        stage_a(0, 0)
         stage_a(0, 1)
-        warm_up(1)
-        stage_b(0)
-        stage_a(1, 0)
         bias_column()
+        stage_b(0)
+        warm_up(1)
+        stage_a(1, 0)
         stage_a(1, 1)
         for it in range(N_GROUPS + 1):
-            if it == 1:
-                rope_tables()
             if it > 0:
                 if it % 2 == 1:
                     stg_new = stp.tile([P, 3, H, JS, HD], F32, name="stg")
                     stg_t[it // 2] = stg_new
-                turn(it - 1, 0)
-                turn(it - 1, 1)
                 rotate(it - 1, 0)
-            if it + 1 < N_GROUPS:
-                stage_b(it + 1)
-            if it > 0:
+                if it + 1 < N_GROUPS:
+                    stage_b(it + 1)
                 rotate(it - 1, 1)
             if it < N_GROUPS:
-                passes(it)
-                for m in range(3):
-                    add_bias(it, m)
-            if it > 0:
+                passes(it, (0, 1))
+                add_bias(it, 0)
+                add_bias(it, 1)
+            if it == 0:
+                rope_tables()
+                stage_b(1)
+            else:
                 turn(it - 1, 2)
                 copy_v(it - 1)
                 stores(it - 1)
             if it + 2 < N_GROUPS:
                 stage_a(it + 2, 0)
+            if it == N_GROUPS - 1:
+                turn(it, 0)
+                turn(it, 1)
+            if it < N_GROUPS:
+                passes(it, (2,))
+                add_bias(it, 2)
+            if it + 2 < N_GROUPS:
                 stage_a(it + 2, 1)
+            if it < N_GROUPS - 1:
+                turn(it, 0)
+                turn(it, 1)

@@ -37,8 +37,8 @@ def tile_causalselfattention_pa_t_kernel(
         mid = ctx.enter_context(tc.tile_pool(name="mid", bufs=3))
         stp = ctx.enter_context(tc.tile_pool(name="stp", bufs=3))
         ps_xt = ctx.enter_context(tc.psum_pool(name="ps_xt", bufs=2))
-        ps_acc = ctx.enter_context(tc.psum_pool(name="ps_acc", bufs=2))
-        ps_o = ctx.enter_context(tc.psum_pool(name="ps_o", bufs=4))
+        ps_acc = ctx.enter_context(tc.psum_pool(name="ps_acc", bufs=3))
+        ps_o = ctx.enter_context(tc.psum_pool(name="ps_o", bufs=3))
 
         b_rows = const.tile([P, P], BF16, name="b_rows")
         nc.vector.memset(b_rows[:], 0.0)
@@ -224,22 +224,28 @@ def tile_causalselfattention_pa_t_kernel(
             j0 = place(g)[2]
             return stg_t[g // 2][:, m, :, j0 : j0 + JG, :].rearrange("p h j d -> p h (j d)")
 
+        each_head = (slice(0, 1), slice(1, 2))
+        both_heads = (slice(0, H),)
+
         def rotate(g, m):
-            u_ps = turned_t[g, m][:].rearrange("p h j d -> p h (j d)")
-            cos_i, sin_i = (
-                rope[:, c, g % SLOTS].rearrange("p h j d -> p h (j d)") for c in range(2)
-            )
-            m1 = mid.tile([P, H, JG * HD], F32, name="m1")
-            m2 = mid.tile([P, H, JG * HD], F32, name="m2")
-            nc.vector.tensor_tensor(out=m1[:], in0=u_ps, in1=cos_i, op=ALU.mult)
+            both = [P, 2, H * JG * HD]
+            prods = mid.tile([P, 2, H, JG, 2, HALF], F32, name="prods")
             nc.vector.tensor_tensor(
-                out=m2[:].rearrange("p h (j f d) -> p h j f d", j=JG, f=2),
-                in0=u_ps.rearrange("p h (j f d) -> p h j f d", j=JG, f=2)[:, :, :, ::-1, :],
-                in1=sin_i.rearrange("p h (j f d) -> p h j f d", j=JG, f=2)[:, :, :, ::-1, :],
+                out=prods[:].rearrange("p c h j f d -> p c (h j f d)"),
+                in0=turned_t[g, m][:].rearrange("p h j d -> p (h j d)").unsqueeze(1).to_broadcast(both),
+                in1=rope[:, :, g % SLOTS].rearrange("p c h j d -> p c (h j d)"),
                 op=ALU.mult,
             )
-            adder = nc.vector if g == N_GROUPS - 1 and m == 1 else nc.gpsimd
-            adder.tensor_tensor(out=staged(g, m), in0=m1[:], in1=m2[:], op=ALU.add)
+            last = g == N_GROUPS - 1 and m == 1
+            adder = nc.vector if last else nc.gpsimd
+            sums = staged(g, m).rearrange("p h (j f d) -> p h j f d", j=JG, f=2)
+            for hs in each_head if last else both_heads:
+                adder.tensor_tensor(
+                    out=sums[:, hs],
+                    in0=prods[:, 0, hs],
+                    in1=prods[:, 1, hs, :, ::-1, :],
+                    op=ALU.add,
+                )
 
         def copy_v(g):
             nc.scalar.copy(out=staged(g, 2), in_=turned_t[g, 2][:].rearrange("p h j d -> p h (j d)"))
@@ -251,11 +257,17 @@ def tile_causalselfattention_pa_t_kernel(
             if g % 2 == 0 and not last_block:
                 return
             ja, jn = (j0, JG) if last_block else (0, JS)
-            for s in (2, 0, 1):
-                dram = outs[s][b, :, blk * P * JS : (blk + 1) * P * JS, :].rearrange(
+            parts = [(2, both_heads), (0, both_heads), (1, both_heads)]
+            if g == N_GROUPS - 1:
+                parts = [(2, both_heads), (1, each_head), (0, both_heads)]
+            for m, heads in parts:
+                dram = outs[m][b, :, blk * P * JS : (blk + 1) * P * JS, :].rearrange(
                     "h (p j) d -> p h j d", j=JS
                 )
-                nc.sync.dma_start(out=dram[:, :, ja : ja + jn, :], in_=stg[:, s, :, ja : ja + jn, :])
+                for hs in heads:
+                    nc.sync.dma_start(
+                        out=dram[:, hs, ja : ja + jn, :], in_=stg[:, m, hs, ja : ja + jn, :]
+                    )
 
         weights()
         stage_a(0, 0)
@@ -287,14 +299,11 @@ def tile_causalselfattention_pa_t_kernel(
                 stores(it - 1)
             if it + 2 < N_GROUPS:
                 stage_a(it + 2, 0)
-            if it == N_GROUPS - 1:
-                turn(it, 0)
-                turn(it, 1)
             if it < N_GROUPS:
                 passes(it, (2,))
                 add_bias(it, 2)
             if it + 2 < N_GROUPS:
                 stage_a(it + 2, 1)
-            if it < N_GROUPS - 1:
+            if it < N_GROUPS:
                 turn(it, 0)
                 turn(it, 1)

from contextlib import ExitStack

import concourse.mybir as mybir
from concourse.masks import make_identity

F32 = mybir.dt.float32
BF16 = mybir.dt.bfloat16
U32 = mybir.dt.uint32
U8 = mybir.dt.uint8
FP8X4 = mybir.dt.float8_e4m3fn_x4
ALU = mybir.AluOpType
ACT = mybir.ActivationFunctionType

P = 128
B, T, D, H, HD = 4, 2048, 512, 2, 64
HALF = HD // 2
FLOPS = 2 * B * T * D * 3 * H * HD

JS = 8
JG = 4
N_GROUPS = B * T // (P * JG)
SLOTS = T // (P * JG)
N_TILES = T // P


def tile_causalselfattention_pa_t_kernel(
    tc, x, rope_cos, rope_sin, qkv_w, qkv_b, out_0, out_1, out_2
):
    nc = tc.nc
    outs = [out_0, out_1, out_2]
    with ExitStack() as ctx:
        ctx.enter_context(tc.manual_schedule())
        const = ctx.enter_context(tc.tile_pool(name="const", bufs=1))
        xin = ctx.enter_context(tc.tile_pool(name="xin", bufs=N_GROUPS))
        grp = ctx.enter_context(tc.tile_pool(name="grp", bufs=3))
        cod = ctx.enter_context(tc.tile_pool(name="cod", bufs=3))
        mid = ctx.enter_context(tc.tile_pool(name="mid", bufs=3))
        stp = ctx.enter_context(tc.tile_pool(name="stp", bufs=3))
        ps_xt = ctx.enter_context(tc.psum_pool(name="ps_xt", bufs=2))
        ps_acc = ctx.enter_context(tc.psum_pool(name="ps_acc", bufs=3))
        ps_o = ctx.enter_context(tc.psum_pool(name="ps_o", bufs=3))

        b_rows = const.tile([P, P], BF16, name="b_rows")
        nc.vector.memset(b_rows[:], 0.0)
        ident = const.tile([P, P], F32, name="ident")
        make_identity(nc, ident[:])

        zeros = const.tile([P, JG * P], BF16, name="zeros")
        nc.vector.memset(zeros[:], 0.0)

        def warm_up(n):
            wm = ps_o.tile([P, H, JG, HD], F32, name="turned")
            for rep in range(n):
                nc.tensor.matmul(
                    wm[:].rearrange("p h j d -> p (h j d)"), lhsT=zeros[:, 0:P], rhs=zeros[:], start=True, stop=True
                )

        warm_up(3)

        x_sb = []

        def load_x(g):
            b, blk, j0 = g // 4, (g // 2) % 2, JG * (g % 2)
            xt_sb = xin.tile([P, JG * D], BF16, name="x_sb")
            rows = x[b, blk * P * JS : (blk + 1) * P * JS, :].rearrange("(p j) k -> p j k", j=JS)
            nc.sync.dma_start(
                out=xt_sb[:].rearrange("p (j k) -> p j k", j=JG), in_=rows[:, j0 : j0 + JG, :]
            )
            x_sb.append((xt_sb[:, 0 : 2 * D], xt_sb[:, 2 * D : 4 * D]))

        def load_x_half(pr):
            half = const.tile([P, 2 * D], BF16, name="x_half%d" % pr)
            rows = x[0, 0 : P * JS, :].rearrange("(p j) k -> p j k", j=JS)
            nc.sync.dma_start(
                out=half[:].rearrange("p (j k) -> p j k", j=2), in_=rows[:, 2 * pr : 2 * pr + 2, :]
            )
            return half[:]

        w_sb = const.tile([P, 3 * D], BF16, name="w_sb")
        nc.sync.dma_start(
            out=w_sb[:].rearrange("f (m k) -> f m k", m=3),
            in_=qkv_w.rearrange("(m f) k -> f m k", m=3),
        )
        x_half0 = load_x_half(0)
        x_half1 = load_x_half(1)
        x_sb.append((x_half0, x_half1))
        nc.sync.dma_start(out=b_rows[0:3, :], in_=qkv_b.rearrange("(m f) -> m f", m=3))
        load_x(1)
        cos_sb = const.tile([P, N_TILES, HD], BF16, name="cos_sb")
        sin_sb = const.tile([P, N_TILES, HD], BF16, name="sin_sb")
        for tab, src in ((cos_sb, rope_cos), (sin_sb, rope_sin)):
            nc.sync.dma_start(
                out=tab[:].rearrange("p (s j) d -> p s j d", s=2),
                in_=src[0, 0].rearrange("(s p j) d -> p s j d", s=2, j=JS),
            )
        for g in range(2, N_GROUPS):
            load_x(g)

        b_f32 = const.tile([P, P], F32, name="b_f32")
        w_words = w_sb[:].bitcast(F32)
        w_grouped = const.tile([P, 3 * P * 4], BF16, name="w_grouped", align_bytes=64)
        wg_words = w_grouped[:].bitcast(F32).rearrange("p (t u) -> p t u", u=2)
        w_codes = const.tile([P, 3 * P], U32, name="w_codes", align_bytes=64)
        w_scales = const.tile([P, 3 * P], U8, name="w_scales", align_bytes=64)

        def weights():
            wt0 = ps_acc.tile([P, 2, 2, P], F32, name="acc")
            wt1 = ps_acc.tile([P, 2, 2, P], F32, name="acc")
            for m in range(3):
                for u in range(2):
                    c0 = m * 256
                    dst = wt0[:, m, u, :] if m < 2 else wt1[:, 0, u, :]
                    nc.tensor.transpose(dst, w_words[:, c0 + u : c0 + 256 : 2], ident[:])
            nc.vector.tensor_copy(
                out=wg_words[:, 0 : 2 * P, :].rearrange("p (j t) u -> p j t u", j=2),
                in_=wt0[:].rearrange("p j u t -> p j t u"),
            )
            nc.scalar.copy(out=wg_words[:, 2 * P : 3 * P, :], in_=wt1[:, 0].rearrange("p u t -> p t u"))
            nc.vector.tensor_copy(out=b_f32[:], in_=b_rows[:])
            nc.vector.quantize_mx(
                out=w_codes[:, 0 : 2 * P].bitcast(FP8X4),
                scales=w_scales[:, 0 : 2 * P],
                in_=w_grouped[:, 0 : 2 * P * 4],
            )
            nc.vector.quantize_mx(
                out=w_codes[:, 2 * P : 3 * P].bitcast(FP8X4),
                scales=w_scales[:, 2 * P : 3 * P],
                in_=w_grouped[:, 2 * P * 4 : 3 * P * 4],
            )

        bias_sb = const.tile([P, 4], F32, name="bias_sb")

        def bias_column():
            bt = ps_acc.tile([P, 2, 2, P], F32, name="acc")
            nc.tensor.transpose(bt[:, 0, 0, :], b_f32[:], ident[:])
            nc.vector.tensor_copy(out=bias_sb[:, 0:3], in_=bt[:, 0, 0, 0:3])

        rope = const.tile([P, 2, SLOTS, H, JG, HD], BF16, name="rope")

        def rope_tables():
            for h in range(H):
                cos_h, sin_h = (rope[:, c, :, h] for c in range(2))
                cos_v, sin_v = (
                    tab[:].rearrange("p (s j) d -> p s j d", s=SLOTS) for tab in (cos_sb, sin_sb)
                )
                nc.vector.tensor_copy(out=cos_h, in_=cos_v)
                nc.vector.tensor_copy(out=sin_h[:, :, :, 0:HALF], in_=sin_v[:, :, :, HALF:HD])
                nc.vector.tensor_scalar_mul(
                    out=sin_h[:, :, :, HALF:HD], in0=sin_v[:, :, :, 0:HALF], scalar1=-1.0
                )

        grouped_t = {}
        codes_t = {}
        acc_t = {}
        biased_t = {}
        turned_t = {}
        stg_t = {}

        def stage_a(g, pr):
            if pr == 0:
                grouped_new = grp.tile([P, JG * P * 4], BF16, name="grouped", align_bytes=64)
                grouped_t[g] = grouped_new
            x_words = x_sb[g][pr].bitcast(F32)
            g_words = grouped_t[g][:].bitcast(F32).rearrange("p (t u) -> p t u", u=2)
            xt = ps_xt.tile([P, 2, 2, P], F32, name="xt")
            for jj in range(2):
                for u in range(2):
                    c0 = jj * 256
                    nc.tensor.transpose(xt[:, jj, u, :], x_words[:, c0 + u : c0 + 256 : 2], ident[:])
            dst = g_words[:, pr * 2 * P : (pr + 1) * 2 * P, :].rearrange("p (j t) u -> p j t u", j=2)
            nc.scalar.copy(out=dst, in_=xt[:].rearrange("p j u t -> p j t u"))

        def stage_b(g):
            codes = cod.tile([P, JG * P], U32, name="codes", align_bytes=64)
            scales = cod.tile([P, JG * P], U8, name="scales", align_bytes=64)
            parts = 2 if g == 0 else 1
            n = JG * P // parts
            for i in range(parts):
                cols = slice(i * n, (i + 1) * n)
                nc.vector.quantize_mx(
                    out=codes[:, cols].bitcast(FP8X4),
                    scales=scales[:, cols],
                    in_=grouped_t[g][:, i * 4 * n : (i + 1) * 4 * n],
                )
            codes_t[g] = (codes, scales)

        def passes(g, ms):
            codes, scales = codes_t[g]
            for m in ms:
                acc = ps_acc.tile([P, JG * P], F32, name="acc")
                nc.tensor.matmul_mx(
                    out=acc[:],
                    lhsT=w_codes[:, m * P : (m + 1) * P].bitcast(FP8X4),
                    lhsT_scale=w_scales[:, m * P : (m + 1) * P],
                    rhs=codes[:].bitcast(FP8X4),
                    rhs_scale=scales[:],
                    start=True,
                    stop=True,
                )
                acc_t[g, m] = acc

        def place(g):
            return g // 4, (g // 2) % 2, JG * (g % 2)

        def add_bias(g, m):
            biased = mid.tile([P, JG * P], F32, name="biased%d" % m)
            if m < 2 or g % 2 == 1 or g == 0:
                nc.scalar.activation(
                    out=biased[:], in_=acc_t[g, m][:], func=ACT.Identity, bias=bias_sb[:, m : m + 1], scale=1.0
                )
            else:
                nc.vector.tensor_scalar_add(
                    out=biased[:], in0=acc_t[g, m][:], scalar1=bias_sb[:, m : m + 1]
                )
            biased_t[g, m] = biased

        def turn(g, m):
            turned = ps_o.tile([P, H, JG, HD], F32, name="turned")
            for jj in range(JG):
                nc.tensor.transpose(turned[:, :, jj, :], biased_t[g, m][:, jj * P : (jj + 1) * P], ident[:])
            turned_t[g, m] = turned

        def staged(g, m):
            j0 = place(g)[2]
            return stg_t[g // 2][:, m, :, j0 : j0 + JG, :].rearrange("p h j d -> p h (j d)")

        each_head = (slice(0, 1), slice(1, 2))
        both_heads = (slice(0, H),)

        def rotate(g, m):
            both = [P, 2, H * JG * HD]
            prods = mid.tile([P, 2, H, JG, 2, HALF], F32, name="prods")
            nc.vector.tensor_tensor(
                out=prods[:].rearrange("p c h j f d -> p c (h j f d)"),
                in0=turned_t[g, m][:].rearrange("p h j d -> p (h j d)").unsqueeze(1).to_broadcast(both),
                in1=rope[:, :, g % SLOTS].rearrange("p c h j d -> p c (h j d)"),
                op=ALU.mult,
            )
            last = g == N_GROUPS - 1 and m == 1
            adder = nc.vector if last else nc.gpsimd
            sums = staged(g, m).rearrange("p h (j f d) -> p h j f d", j=JG, f=2)
            for hs in each_head if last else both_heads:
                adder.tensor_tensor(
                    out=sums[:, hs],
                    in0=prods[:, 0, hs],
                    in1=prods[:, 1, hs, :, ::-1, :],
                    op=ALU.add,
                )

        def copy_v(g):
            nc.scalar.copy(out=staged(g, 2), in_=turned_t[g, 2][:].rearrange("p h j d -> p h (j d)"))

        def stores(g):
            b, blk, j0 = place(g)
            stg = stg_t[g // 2]
            last_block = g // 2 == N_GROUPS // 2 - 1
            if g % 2 == 0 and not last_block:
                return
            ja, jn = (j0, JG) if last_block else (0, JS)
            parts = [(2, both_heads), (0, both_heads), (1, both_heads)]
            if g == N_GROUPS - 1:
                parts = [(2, both_heads), (1, each_head), (0, both_heads)]
            for m, heads in parts:
                dram = outs[m][b, :, blk * P * JS : (blk + 1) * P * JS, :].rearrange(
                    "h (p j) d -> p h j d", j=JS
                )
                for hs in heads:
                    nc.sync.dma_start(
                        out=dram[:, hs, ja : ja + jn, :], in_=stg[:, m, hs, ja : ja + jn, :]
                    )

        weights()
        stage_a(0, 0)
        stage_a(0, 1)
        bias_column()
        stage_b(0)
        warm_up(1)
        stage_a(1, 0)
        stage_a(1, 1)
        for it in range(N_GROUPS + 1):
            if it > 0:
                if it % 2 == 1:
                    stg_new = stp.tile([P, 3, H, JS, HD], F32, name="stg")
                    stg_t[it // 2] = stg_new
                rotate(it - 1, 0)
                if it + 1 < N_GROUPS:
                    stage_b(it + 1)
                rotate(it - 1, 1)
            if it < N_GROUPS:
                passes(it, (0, 1))
                add_bias(it, 0)
                add_bias(it, 1)
            if it == 0:
                rope_tables()
                stage_b(1)
            else:
                turn(it - 1, 2)
                copy_v(it - 1)
                stores(it - 1)
            if it + 2 < N_GROUPS:
                stage_a(it + 2, 0)
            if it < N_GROUPS:
                passes(it, (2,))
                add_bias(it, 2)
            if it + 2 < N_GROUPS:
                stage_a(it + 2, 1)
            if it < N_GROUPS:
                turn(it, 0)
                turn(it, 1)
